import numpy as np
import ml_dtypes


def mxq(x, axis, fmt="e4m3"):
    dtype, down = {"e4m3": (ml_dtypes.float8_e4m3fn, 7), "e5m2": (ml_dtypes.float8_e5m2, 14)}[fmt]
    v = np.moveaxis(np.asarray(x, np.float32).astype(ml_dtypes.bfloat16).astype(np.float64), axis, -1)
    blocks = v.reshape(v.shape[:-1] + (-1, 32))
    amax = np.abs(blocks).max(-1, keepdims=True)
    byte = np.maximum(np.where(amax > 0, np.frexp(amax)[1] - 1 + 127, 0) - down, 1)
    scale = np.exp2(byte - 127.0)
    codes = (blocks / scale).astype(np.float32).astype(dtype).astype(np.float64)
    return np.moveaxis((codes * scale).reshape(v.shape), -1, axis)


WIDE = False


def mx_kscale(k):
    if not WIDE:
        return np.ones(k)
    levels = np.array([10, -10, 5, -5, 0])
    if k % 512:
        return np.exp2(np.random.permutation(np.resize(levels, k // 32))).repeat(32)
    a = np.empty((k // 512, 16))
    for p in range(k // 512):
        a[p, :8] = np.random.permutation(np.resize(levels, 8))
        for g in range(8):
            far = levels[np.abs(levels - a[p, g]) >= 10]
            a[p, g + 8] = far[np.random.randint(len(far))]
    return np.exp2(a.ravel()).repeat(32)


BF16 = ml_dtypes.bfloat16


def bf(x):
    return np.asarray(x, np.float32).astype(BF16)


def f64(x):
    return np.asarray(x).astype(np.float64)


B, STACK, TUBE, CH, IMG, PATCH, EMBED = 20, 16, 4, 1, 128, 16, 1024
GH = IMG // PATCH
GW = IMG // PATCH
GD = STACK // TUBE
K = TUBE * CH * PATCH * PATCH


def _sincos_1d(dim, pos):
    omega = 1.0 / (10000.0 ** (np.arange(dim // 2, dtype=np.float64) / (dim / 2.0)))
    out = pos[:, None].astype(np.float64) * omega[None, :]
    return np.concatenate([np.sin(out), np.cos(out)], axis=1)


def get_3d_sincos_pos_embed(grid_h, grid_w, grid_depth, embed_dim):
    dim_t = embed_dim // 4
    dim_s = embed_dim - dim_t
    emb_t = _sincos_1d(dim_t, np.arange(grid_depth))
    emb_h = _sincos_1d(dim_s // 2, np.arange(grid_h))
    emb_w = _sincos_1d(dim_s - dim_s // 2, np.arange(grid_w))
    emb_hw = np.concatenate([np.repeat(emb_h, grid_w, axis=0), np.tile(emb_w, (grid_h, 1))], axis=1)
    ns = grid_h * grid_w
    return np.concatenate([np.repeat(emb_t, ns, axis=0), np.tile(emb_hw, (grid_depth, 1))], axis=1)


def setup_inputs():
    s = mx_kscale(K)
    sv = s.reshape(TUBE, CH, PATCH, PATCH)[:, :, None, :, None, :]
    video = np.random.standard_normal((B, GD, TUBE, CH, GH, PATCH, GW, PATCH)) * sv
    return {"video": bf(video.reshape(B, STACK, CH, IMG, IMG)),
            "W": bf(np.random.standard_normal((EMBED, K)) / np.sqrt(K) / s[None, :]),
            "b": bf(np.random.standard_normal(EMBED) * 0.3),
            "pos_embed": bf(get_3d_sincos_pos_embed(GH, GW, GD, EMBED)[None])}


def reference(video, W, b, pos_embed):
    video = f64(video)
    B_, T, C, H, W_ = video.shape
    p = PATCH
    gh, gw = H // p, W_ // p
    ns = gh * gw
    x = video.reshape(B_ * T, C, gh, p, gw, p)
    x = x.transpose(0, 2, 4, 1, 3, 5)
    x = x.reshape(B_, T, ns, C * p * p)
    x = x.reshape(B_, GD, TUBE, ns, C * p * p)
    x = x.transpose(0, 1, 3, 2, 4)
    tubelets = x.reshape(B_, GD * ns, TUBE * C * p * p)
    tokens = (mxq(tubelets, 2, "e4m3") @ mxq(f64(W), 1, "e4m3").T) + f64(b) + f64(pos_embed)
    return tokens

@@ -1,0 +1,257 @@
+from contextlib import ExitStack
+
+import concourse.mybir as mybir
+from concourse.masks import make_identity
+
+F32 = mybir.dt.float32
+BF16 = mybir.dt.bfloat16
+I32 = mybir.dt.int32
+U32 = mybir.dt.uint32
+U8 = mybir.dt.uint8
+FP8X4 = mybir.dt.float8_e4m3fn_x4
+ADD = mybir.AluOpType.add
+
+P = 128
+NB = 20
+EMB = 1024
+FLOPS = 2 * NB * 256 * 1024 * EMB
+
+W_CHUNKS = [(0, 2), (256, 2), (512, 2), (768, 1), (896, 1)]
+FINE_STORES_FROM = 16
+GROUPS = [[x, x + 1] for x in range(0, NB, 2)]
+
+
+def tile_tubeletembedding_t_kernel(tc, video, W, b, pos_embed, out):
+    nc = tc.nc
+    with ExitStack() as ctx:
+        ctx.enter_context(tc.manual_schedule())
+        const = ctx.enter_context(tc.tile_pool(name="const", bufs=1))
+        vids = ctx.enter_context(tc.tile_pool(name="vids", bufs=1))
+        work = ctx.enter_context(tc.tile_pool(name="work", bufs=3))
+        resp = ctx.enter_context(tc.tile_pool(name="resp", bufs=7))
+        pst = ctx.enter_context(tc.psum_pool(name="pst", bufs=4))
+        psa = ctx.enter_context(tc.psum_pool(name="psa", bufs=4))
+
+        brow = const.tile([P, EMB], BF16, name="brow")
+        nc.vector.memset(brow[:].bitcast(I32), 0)
+        ones = const.tile([P, P], BF16, name="ones")
+        nc.vector.memset(ones[:], 1.0)
+        ident = const.tile([P, P], F32, name="ident")
+        make_identity(nc, ident[:])
+        perm = const.tile([P, P], F32, name="perm")
+        nc.vector.tensor_copy(
+            out=perm[:].rearrange("p (g x i) -> p g x i", g=2, x=8, i=8),
+            in_=ident[:].rearrange("p (x g i) -> p g x i", g=2, x=8, i=8),
+        )
+
+        raw = {}
+
+        def load_pair(b0):
+            t = vids.tile([P, 4096], BF16, name="vid%d" % b0)
+            frames = video[b0 : b0 + 2].rearrange(
+                "b (y tl) c (i py) w -> tl b y c i (py w)", tl=2, py=16
+            )
+            for tl in range(2):
+                nc.sync.dma_start(
+                    out=t[:, tl * 2048 : (tl + 1) * 2048],
+                    in_=frames[tl].rearrange("b y c i f -> (b y) (c i) f"),
+                )
+            raw[b0] = t
+
+        w_raw = []
+
+        def load_w(c):
+            row0, n_eb = W_CHUNKS[c]
+            t = resp.tile([P, n_eb, 1024], BF16, name="wraw%d" % c, tag="res", align_bytes=64)
+            nc.sync.dma_start(
+                out=t[:],
+                in_=W[row0 : row0 + n_eb * P, :].rearrange("(p eb) k -> p eb k", eb=n_eb),
+            )
+            w_raw.append(t)
+
+        load_pair(0)
+        nc.sync.dma_start(out=brow[0:1, :], in_=b.rearrange("(o e) -> o e", o=1))
+        for c in range(len(W_CHUNKS)):
+            load_w(c)
+        pos_raw = const.tile([P, 2, EMB], BF16, name="pos_raw")
+        nc.sync.dma_start(out=pos_raw[:], in_=pos_embed[0].rearrange("(m J) e -> m J e", J=2))
+        for b0 in range(2, NB, 2):
+            load_pair(b0)
+
+        w_grp = [
+            resp.tile([P, 4 * EMB], BF16, name="w_grp%d" % g, tag="res", align_bytes=64)
+            for g in range(2)
+        ]
+        w_code = const.tile([P, 2, EMB], U32, name="w_code", align_bytes=64)
+        w_scale = const.tile([P, 2, EMB], U8, name="w_scale", align_bytes=64)
+        bias_bc = const.tile([P, EMB], F32, name="bias_bc")
+        posb = const.tile([P, 2, EMB], F32, name="posb")
+
+        re_t = {}
+        grp_t = {}
+        code_t = {}
+
+        def copy(eng, dst, src):
+            if eng == "v":
+                nc.vector.tensor_copy(out=dst, in_=src)
+            else:
+                nc.scalar.copy(out=dst, in_=src)
+
+        def stage_e(b0, engs):
+            re = work.tile([P, 2048], F32, name="re", bufs=2)
+            for u in range(2):
+                copy(
+                    engs[u],
+                    re[:].rearrange("p (j u x q) -> p u j x q", j=8, u=2, x=32, q=4)[:, u],
+                    raw[b0][:].bitcast(F32).rearrange("p (x j q u) -> p u j x q", x=32, j=8, q=4, u=2)[:, u],
+                )
+            re_t[b0] = re
+
+        def stage_t(b0, engs):
+            grp = work.tile([P, 4096], BF16, name="grp", bufs=2, align_bytes=64)
+            grp_t[b0] = grp
+            dst_all = grp[:].bitcast(F32).rearrange(
+                "p (J x yh yl u) -> p J yh x yl u", J=2, x=P, yh=2, yl=2, u=2
+            )
+            re = re_t[b0]
+            for J in range(2):
+                for yh in range(2):
+                    tp = pst.tile([P, 512], F32, name="tp")
+                    for yl in range(2):
+                        for u in range(2):
+                            j = 4 * yh + 2 * yl + J
+                            nc.tensor.transpose(
+                                tp[:, (2 * yl + u) * P : (2 * yl + u + 1) * P],
+                                re[:, (2 * j + u) * P : (2 * j + u + 1) * P],
+                                perm[:],
+                            )
+                    copy(
+                        engs[yh],
+                        dst_all[:, J, yh],
+                        tp[:].rearrange("p (yl u x) -> p x yl u", yl=2, u=2, x=P),
+                    )
+
+        def stage_q(b0):
+            xc = work.tile([P, 1024], U32, name="xc", align_bytes=64)
+            xs = work.tile([P, 1024], U8, name="xs", align_bytes=64)
+            for J in range(2):
+                nc.vector.quantize_mx(
+                    out=xc[:, J * 512 : (J + 1) * 512].bitcast(FP8X4),
+                    scales=xs[:, J * 512 : (J + 1) * 512],
+                    in_=grp_t[b0][:, J * 2048 : (J + 1) * 2048],
+                )
+            for bb in range(2):
+                code_t[b0 + bb] = (xc, xs, bb)
+
+        def stage_w(c, engs):
+            row0, n_eb = W_CHUNKS[c]
+            wf = w_raw[c][:].bitcast(F32)
+            width = 2 * n_eb * P
+            for g in range(2):
+                tp = pst.tile([P, 512], F32, name="tp")
+                for u in range(2):
+                    for ebl in range(n_eb):
+                        q = u * n_eb + ebl
+                        nc.tensor.transpose(
+                            tp[:, q * P : (q + 1) * P],
+                            wf[:, ebl, g * 256 + u : (g + 1) * 256 : 2],
+                            ident[:],
+                        )
+                copy(
+                    engs[g],
+                    w_grp[g][:].bitcast(F32)[:, row0 * 2 : row0 * 2 + width].rearrange(
+                        "p (e eb u) -> p e eb u", eb=n_eb, u=2
+                    ),
+                    tp[:, 0:width].rearrange("p (u eb e) -> p e eb u", u=2, eb=n_eb),
+                )
+
+        def stage_wq(c):
+            row0, n_eb = W_CHUNKS[c]
+            n = n_eb * P
+            for g in range(2):
+                nc.vector.quantize_mx(
+                    out=w_code[:, g, row0 : row0 + n].bitcast(FP8X4),
+                    scales=w_scale[:, g, row0 : row0 + n],
+                    in_=w_grp[g][:, row0 * 4 : (row0 + n) * 4],
+                )
+
+        res_t = {}
+        acc_t = {}
+
+        def mm(bi, J, eh):
+            xc, xs, bb = code_t[bi]
+            acc = psa.tile([P, 512], F32, name="acc")
+            acc_t[(bi, J, eh)] = acc
+            cols = slice(eh * 512, (eh + 1) * 512)
+            for g in range(2):
+                blk = (J * 2 + g) * 2 + bb
+                m = slice(blk * P, (blk + 1) * P)
+                nc.tensor.matmul_mx(
+                    out=acc[:],
+                    lhsT=xc[:, m].bitcast(FP8X4),
+                    lhsT_scale=xs[:, m],
+                    rhs=w_code[:, g, cols].bitcast(FP8X4),
+                    rhs_scale=w_scale[:, g, cols],
+                    start=(g == 0),
+                    stop=(g == 1),
+                )
+
+        def add_store(bi, J, eh):
+            if (J, eh) == (0, 0):
+                res_t[bi] = resp.tile([P, 2, EMB], F32, name="res", tag="res", align_bytes=64)
+            res = res_t[bi]
+            cols = slice(eh * 512, (eh + 1) * 512)
+            nc.vector.tensor_tensor(
+                out=res[:, J, cols], in0=acc_t[(bi, J, eh)][:], in1=posb[:, J, cols], op=ADD
+            )
+            dram = out[bi].rearrange("(m J) e -> m J e", J=2)
+            if bi >= FINE_STORES_FROM:
+                if eh == 1:
+                    nc.sync.dma_start(out=dram[:, J, :], in_=res[:, J, :])
+            elif (J, eh) == (1, 1):
+                nc.sync.dma_start(out=dram, in_=res[:])
+
+        def posb_piece(eng, J, eh):
+            cols = slice(eh * 512, (eh + 1) * 512)
+            eng.tensor_tensor(
+                out=posb[:, J, cols], in0=pos_raw[:, J, cols], in1=bias_bc[:, cols], op=ADD
+            )
+
+        for eh in range(2):
+            cols = slice(eh * 512, (eh + 1) * 512)
+            acc = psa.tile([P, 512], F32, name="acc")
+            nc.tensor.matmul(out=acc[:], lhsT=ones[:], rhs=brow[:, cols], start=True, stop=True)
+            nc.scalar.copy(out=bias_bc[:, cols], in_=acc[:])
+        stage_e(0, "vs")
+        stage_t(0, "vs")
+        stage_q(0)
+        stage_w(0, "vs")
+        stage_w(1, "ss")
+        stage_wq(0)
+        stage_w(2, "ss")
+        stage_wq(1)
+        stage_w(3, "vs")
+        stage_wq(2)
+        stage_w(4, "vs")
+        stage_wq(3)
+        stage_wq(4)
+        stage_e(2, "ss")
+        posb_piece(nc.vector, 0, 0)
+        posb_piece(nc.vector, 0, 1)
+        posb_piece(nc.gpsimd, 1, 0)
+        posb_piece(nc.gpsimd, 1, 1)
+
+        for k in range(1, len(GROUPS) + 1):
+            g_now = GROUPS[k][0] if k < len(GROUPS) else None
+            banks = [(bi, J, eh) for bi in GROUPS[k - 1] for J in range(2) for eh in range(2)]
+            if k > 1 and g_now is not None:
+                stage_t(g_now, "ss")
+            for n, bk in enumerate(banks):
+                if n == 4 and k == 1:
+                    stage_t(g_now, "ss")
+                if n == 4 and k + 1 < len(GROUPS):
+                    stage_e(GROUPS[k + 1][0], "ss")
+                if n == 6 and g_now is not None:
+                    stage_q(g_now)
+                mm(bk[0], bk[1], bk[2])
+                add_store(bk[0], bk[1], bk[2])

@@ -99,11 +99,11 @@ def tile_tubeletembedding_t_kernel(tc, video, W, b, pos_embed, out):
 
         def stage_e(b0, engs):
             re = work.tile([P, 2048], F32, name="re", bufs=2)
-            for u in range(2):
+            for j in range(8):
                 copy(
-                    engs[u],
-                    re[:].rearrange("p (j u x q) -> p u j x q", j=8, u=2, x=32, q=4)[:, u],
-                    raw[b0][:].bitcast(F32).rearrange("p (x j q u) -> p u j x q", x=32, j=8, q=4, u=2)[:, u],
+                    engs[j % 2],
+                    re[:, j * 256 : (j + 1) * 256].rearrange("p (u x q) -> p x q u", u=2, x=32, q=4),
+                    raw[b0][:].bitcast(F32).rearrange("p (x j q u) -> p j x q u", x=32, j=8, q=4, u=2)[:, j],
                 )
             re_t[b0] = re
 
@@ -111,7 +111,7 @@ def tile_tubeletembedding_t_kernel(tc, video, W, b, pos_embed, out):
             grp = work.tile([P, 4096], BF16, name="grp", bufs=2, align_bytes=64)
             grp_t[b0] = grp
             dst_all = grp[:].bitcast(F32).rearrange(
-                "p (J x yh yl u) -> p J yh x yl u", J=2, x=P, yh=2, yl=2, u=2
+                "p (J x i yh t) -> p J yh x t i", J=2, x=64, i=2, yh=2, t=4
             )
             re = re_t[b0]
             for J in range(2):
@@ -128,7 +128,7 @@ def tile_tubeletembedding_t_kernel(tc, video, W, b, pos_embed, out):
                     copy(
                         engs[yh],
                         dst_all[:, J, yh],
-                        tp[:].rearrange("p (yl u x) -> p x yl u", yl=2, u=2, x=P),
+                        tp[:].rearrange("p (t x i) -> p x t i", t=4, x=64, i=2),
                     )
 
         def stage_q(b0):

@@ -46,13 +46,13 @@ def tile_tubeletembedding_t_kernel(tc, video, W, b, pos_embed, out):
 
         raw = {}
 
-        def load_pair(b0):
+        def load_pair(b0, queue):
             t = vids.tile([P, 4096], BF16, name="vid%d" % b0)
             frames = video[b0 : b0 + 2].rearrange(
                 "b (y tl) c (i py) w -> tl b y c i (py w)", tl=2, py=16
             )
             for tl in range(2):
-                nc.sync.dma_start(
+                queue.dma_start(
                     out=t[:, tl * 2048 : (tl + 1) * 2048],
                     in_=frames[tl].rearrange("b y c i f -> (b y) (c i) f"),
                 )
@@ -69,14 +69,13 @@ def tile_tubeletembedding_t_kernel(tc, video, W, b, pos_embed, out):
             )
             w_raw.append(t)
 
-        load_pair(0)
+        load_pair(0, nc.sync)
         nc.sync.dma_start(out=brow[0:1, :], in_=b.rearrange("(o e) -> o e", o=1))
         for c in range(len(W_CHUNKS)):
             load_w(c)
         pos_raw = const.tile([P, 2, EMB], BF16, name="pos_raw")
         nc.sync.dma_start(out=pos_raw[:], in_=pos_embed[0].rearrange("(m J) e -> m J e", J=2))
-        for b0 in range(2, NB, 2):
-            load_pair(b0)
+        load_pair(2, nc.sync)
 
         w_grp = [
             resp.tile([P, 4 * EMB], BF16, name="w_grp%d" % g, tag="res", align_bytes=64)
@@ -240,6 +239,8 @@ def tile_tubeletembedding_t_kernel(tc, video, W, b, pos_embed, out):
         posb_piece(nc.vector, 0, 1)
         posb_piece(nc.gpsimd, 1, 0)
         posb_piece(nc.gpsimd, 1, 1)
+        for b0 in range(4, NB, 2):
+            load_pair(b0, nc.gpsimd)
 
         for k in range(1, len(GROUPS) + 1):
             g_now = GROUPS[k][0] if k < len(GROUPS) else None

@@ -106,29 +106,29 @@ def tile_tubeletembedding_t_kernel(tc, video, W, b, pos_embed, out):
                 )
             re_t[b0] = re
 
-        def stage_t(b0, engs):
-            grp = work.tile([P, 4096], BF16, name="grp", bufs=2, align_bytes=64)
-            grp_t[b0] = grp
+        def stage_t(b0, J, engs):
+            if J == 0:
+                grp_t[b0] = work.tile([P, 4096], BF16, name="grp", bufs=2, align_bytes=64)
+            grp = grp_t[b0]
             dst_all = grp[:].bitcast(F32).rearrange(
                 "p (J x i yh t) -> p J yh x t i", J=2, x=64, i=2, yh=2, t=4
             )
             re = re_t[b0]
-            for J in range(2):
-                for yh in range(2):
-                    tp = pst.tile([P, 512], F32, name="tp")
-                    for yl in range(2):
-                        for u in range(2):
-                            j = 4 * yh + 2 * yl + J
-                            nc.tensor.transpose(
-                                tp[:, (2 * yl + u) * P : (2 * yl + u + 1) * P],
-                                re[:, (2 * j + u) * P : (2 * j + u + 1) * P],
-                                perm[:],
-                            )
-                    copy(
-                        engs[yh],
-                        dst_all[:, J, yh],
-                        tp[:].rearrange("p (t x i) -> p x t i", t=4, x=64, i=2),
-                    )
+            for yh in range(2):
+                tp = pst.tile([P, 512], F32, name="tp")
+                for yl in range(2):
+                    for u in range(2):
+                        j = 4 * yh + 2 * yl + J
+                        nc.tensor.transpose(
+                            tp[:, (2 * yl + u) * P : (2 * yl + u + 1) * P],
+                            re[:, (2 * j + u) * P : (2 * j + u + 1) * P],
+                            perm[:],
+                        )
+                copy(
+                    engs[yh],
+                    dst_all[:, J, yh],
+                    tp[:].rearrange("p (t x i) -> p x t i", t=4, x=64, i=2),
+                )
 
         def stage_q(b0):
             xc = work.tile([P, 1024], U32, name="xc", align_bytes=64)
@@ -222,7 +222,8 @@ def tile_tubeletembedding_t_kernel(tc, video, W, b, pos_embed, out):
             nc.tensor.matmul(out=acc[:], lhsT=ones[:], rhs=brow[:, cols], start=True, stop=True)
             nc.scalar.copy(out=bias_bc[:, cols], in_=acc[:])
         stage_e(0, "vs")
-        stage_t(0, "vs")
+        for J in range(2):
+            stage_t(0, J, "vs")
         stage_q(0)
         stage_w(0, "vs")
         stage_w(1, "ss")
@@ -246,10 +247,11 @@ def tile_tubeletembedding_t_kernel(tc, video, W, b, pos_embed, out):
             g_now = GROUPS[k][0] if k < len(GROUPS) else None
             banks = [(bi, J, eh) for bi in GROUPS[k - 1] for J in range(2) for eh in range(2)]
             if k > 1 and g_now is not None:
-                stage_t(g_now, "ss")
+                stage_t(g_now, 0, "ss")
             for n, bk in enumerate(banks):
-                if n == 4 and k == 1:
-                    stage_t(g_now, "ss")
+                if n == (4 if k == 1 else 2) and g_now is not None:
+                    for J in range(0 if k == 1 else 1, 2):
+                        stage_t(g_now, J, "ss")
                 if n == 4 and k + 1 < len(GROUPS):
                     stage_e(GROUPS[k + 1][0], "ss")
                 if n == 6 and g_now is not None:

from contextlib import ExitStack

import concourse.mybir as mybir
from concourse.masks import make_identity

F32 = mybir.dt.float32
BF16 = mybir.dt.bfloat16
I32 = mybir.dt.int32
U32 = mybir.dt.uint32
U8 = mybir.dt.uint8
FP8X4 = mybir.dt.float8_e4m3fn_x4
ADD = mybir.AluOpType.add

P = 128
NB = 20
EMB = 1024
FLOPS = 2 * NB * 256 * 1024 * EMB

W_CHUNKS = [(0, 2), (256, 2), (512, 2), (768, 1), (896, 1)]
FINE_STORES_FROM = 16
GROUPS = [[x, x + 1] for x in range(0, NB, 2)]


def tile_tubeletembedding_t_kernel(tc, video, W, b, pos_embed, out):
    nc = tc.nc
    with ExitStack() as ctx:
        ctx.enter_context(tc.manual_schedule())
        const = ctx.enter_context(tc.tile_pool(name="const", bufs=1))
        vids = ctx.enter_context(tc.tile_pool(name="vids", bufs=1))
        work = ctx.enter_context(tc.tile_pool(name="work", bufs=3))
        resp = ctx.enter_context(tc.tile_pool(name="resp", bufs=7))
        pst = ctx.enter_context(tc.psum_pool(name="pst", bufs=4))
        psa = ctx.enter_context(tc.psum_pool(name="psa", bufs=4))

        brow = const.tile([P, EMB], BF16, name="brow")
        nc.vector.memset(brow[:].bitcast(I32), 0)
        ones = const.tile([P, P], BF16, name="ones")
        nc.vector.memset(ones[:], 1.0)
        ident = const.tile([P, P], F32, name="ident")
        make_identity(nc, ident[:])
        perm = const.tile([P, P], F32, name="perm")
        nc.vector.tensor_copy(
            out=perm[:].rearrange("p (g x i) -> p g x i", g=2, x=8, i=8),
            in_=ident[:].rearrange("p (x g i) -> p g x i", g=2, x=8, i=8),
        )

        raw = {}

        def load_pair(b0, queue):
            t = vids.tile([P, 4096], BF16, name="vid%d" % b0)
            frames = video[b0 : b0 + 2].rearrange(
                "b (y tl) c (i py) w -> tl b y c i (py w)", tl=2, py=16
            )
            for tl in range(2):
                queue.dma_start(
                    out=t[:, tl * 2048 : (tl + 1) * 2048],
                    in_=frames[tl].rearrange("b y c i f -> (b y) (c i) f"),
                )
            raw[b0] = t

        w_raw = []

        def load_w(c):
            row0, n_eb = W_CHUNKS[c]
            t = resp.tile([P, n_eb, 1024], BF16, name="wraw%d" % c, tag="res", align_bytes=64)
            nc.sync.dma_start(
                out=t[:],
                in_=W[row0 : row0 + n_eb * P, :].rearrange("(p eb) k -> p eb k", eb=n_eb),
            )
            w_raw.append(t)

        load_pair(0, nc.sync)
        nc.sync.dma_start(out=brow[0:1, :], in_=b.rearrange("(o e) -> o e", o=1))
        for c in range(len(W_CHUNKS)):
            load_w(c)
        pos_raw = const.tile([P, 2, EMB], BF16, name="pos_raw")
        nc.sync.dma_start(out=pos_raw[:], in_=pos_embed[0].rearrange("(m J) e -> m J e", J=2))
        load_pair(2, nc.sync)

        w_grp = [
            resp.tile([P, 4 * EMB], BF16, name="w_grp%d" % g, tag="res", align_bytes=64)
            for g in range(2)
        ]
        w_code = const.tile([P, 2, EMB], U32, name="w_code", align_bytes=64)
        w_scale = const.tile([P, 2, EMB], U8, name="w_scale", align_bytes=64)
        bias_bc = const.tile([P, EMB], F32, name="bias_bc")
        posb = const.tile([P, 2, EMB], F32, name="posb")

        re_t = {}
        grp_t = {}
        code_t = {}

        def copy(eng, dst, src):
            if eng == "v":
                nc.vector.tensor_copy(out=dst, in_=src)
            else:
                nc.scalar.copy(out=dst, in_=src)

        def stage_e(b0, engs):
            re = work.tile([P, 2048], F32, name="re", bufs=2)
            for j in range(8):
                copy(
                    engs[j % 2],
                    re[:, j * 256 : (j + 1) * 256].rearrange("p (u x q) -> p x q u", u=2, x=32, q=4),
                    raw[b0][:].bitcast(F32).rearrange("p (x j q u) -> p j x q u", x=32, j=8, q=4, u=2)[:, j],
                )
            re_t[b0] = re

        def stage_t(b0, J, engs):
            if J == 0:
                grp_t[b0] = work.tile([P, 4096], BF16, name="grp", bufs=2, align_bytes=64)
            grp = grp_t[b0]
            dst_all = grp[:].bitcast(F32).rearrange(
                "p (J x i yh t) -> p J yh x t i", J=2, x=64, i=2, yh=2, t=4
            )
            re = re_t[b0]
            for yh in range(2):
                tp = pst.tile([P, 512], F32, name="tp")
                for yl in range(2):
                    for u in range(2):
                        j = 4 * yh + 2 * yl + J
                        nc.tensor.transpose(
                            tp[:, (2 * yl + u) * P : (2 * yl + u + 1) * P],
                            re[:, (2 * j + u) * P : (2 * j + u + 1) * P],
                            perm[:],
                        )
                copy(
                    engs[yh],
                    dst_all[:, J, yh],
                    tp[:].rearrange("p (t x i) -> p x t i", t=4, x=64, i=2),
                )

        def stage_q(b0):
            xc = work.tile([P, 1024], U32, name="xc", align_bytes=64)
            xs = work.tile([P, 1024], U8, name="xs", align_bytes=64)
            for J in range(2):
                nc.vector.quantize_mx(
                    out=xc[:, J * 512 : (J + 1) * 512].bitcast(FP8X4),
                    scales=xs[:, J * 512 : (J + 1) * 512],
                    in_=grp_t[b0][:, J * 2048 : (J + 1) * 2048],
                )
            for bb in range(2):
                code_t[b0 + bb] = (xc, xs, bb)

        def stage_w(c, engs):
            row0, n_eb = W_CHUNKS[c]
            wf = w_raw[c][:].bitcast(F32)
            width = 2 * n_eb * P
            for g in range(2):
                tp = pst.tile([P, 512], F32, name="tp")
                for u in range(2):
                    for ebl in range(n_eb):
                        q = u * n_eb + ebl
                        nc.tensor.transpose(
                            tp[:, q * P : (q + 1) * P],
                            wf[:, ebl, g * 256 + u : (g + 1) * 256 : 2],
                            ident[:],
                        )
                copy(
                    engs[g],
                    w_grp[g][:].bitcast(F32)[:, row0 * 2 : row0 * 2 + width].rearrange(
                        "p (e eb u) -> p e eb u", eb=n_eb, u=2
                    ),
                    tp[:, 0:width].rearrange("p (u eb e) -> p e eb u", u=2, eb=n_eb),
                )

        def stage_wq(c):
            row0, n_eb = W_CHUNKS[c]
            n = n_eb * P
            for g in range(2):
                nc.vector.quantize_mx(
                    out=w_code[:, g, row0 : row0 + n].bitcast(FP8X4),
                    scales=w_scale[:, g, row0 : row0 + n],
                    in_=w_grp[g][:, row0 * 4 : (row0 + n) * 4],
                )

        res_t = {}
        acc_t = {}

        def mm(bi, J, eh):
            xc, xs, bb = code_t[bi]
            acc = psa.tile([P, 512], F32, name="acc")
            acc_t[(bi, J, eh)] = acc
            cols = slice(eh * 512, (eh + 1) * 512)
            for g in range(2):
                blk = (J * 2 + g) * 2 + bb
                m = slice(blk * P, (blk + 1) * P)
                nc.tensor.matmul_mx(
                    out=acc[:],
                    lhsT=xc[:, m].bitcast(FP8X4),
                    lhsT_scale=xs[:, m],
                    rhs=w_code[:, g, cols].bitcast(FP8X4),
                    rhs_scale=w_scale[:, g, cols],
                    start=(g == 0),
                    stop=(g == 1),
                )

        def add_store(bi, J, eh):
            if (J, eh) == (0, 0):
                res_t[bi] = resp.tile([P, 2, EMB], F32, name="res", tag="res", align_bytes=64)
            res = res_t[bi]
            cols = slice(eh * 512, (eh + 1) * 512)
            nc.vector.tensor_tensor(
                out=res[:, J, cols], in0=acc_t[(bi, J, eh)][:], in1=posb[:, J, cols], op=ADD
            )
            dram = out[bi].rearrange("(m J) e -> m J e", J=2)
            if bi >= FINE_STORES_FROM:
                if eh == 1:
                    nc.sync.dma_start(out=dram[:, J, :], in_=res[:, J, :])
            elif (J, eh) == (1, 1):
                nc.sync.dma_start(out=dram, in_=res[:])

        def posb_piece(eng, J, eh):
            cols = slice(eh * 512, (eh + 1) * 512)
            eng.tensor_tensor(
                out=posb[:, J, cols], in0=pos_raw[:, J, cols], in1=bias_bc[:, cols], op=ADD
            )

        for eh in range(2):
            cols = slice(eh * 512, (eh + 1) * 512)
            acc = psa.tile([P, 512], F32, name="acc")
            nc.tensor.matmul(out=acc[:], lhsT=ones[:], rhs=brow[:, cols], start=True, stop=True)
            nc.scalar.copy(out=bias_bc[:, cols], in_=acc[:])
        stage_e(0, "vs")
        for J in range(2):
            stage_t(0, J, "vs")
        stage_q(0)
        stage_w(0, "vs")
        stage_w(1, "ss")
        stage_wq(0)
        stage_w(2, "ss")
        stage_wq(1)
        stage_w(3, "vs")
        stage_wq(2)
        stage_w(4, "vs")
        stage_wq(3)
        stage_wq(4)
        stage_e(2, "ss")
        posb_piece(nc.vector, 0, 0)
        posb_piece(nc.vector, 0, 1)
        posb_piece(nc.gpsimd, 1, 0)
        posb_piece(nc.gpsimd, 1, 1)
        for b0 in range(4, NB, 2):
            load_pair(b0, nc.gpsimd)

        for k in range(1, len(GROUPS) + 1):
            g_now = GROUPS[k][0] if k < len(GROUPS) else None
            banks = [(bi, J, eh) for bi in GROUPS[k - 1] for J in range(2) for eh in range(2)]
            if k > 1 and g_now is not None:
                stage_t(g_now, 0, "ss")
            for n, bk in enumerate(banks):
                if n == (4 if k == 1 else 2) and g_now is not None:
                    for J in range(0 if k == 1 else 1, 2):
                        stage_t(g_now, J, "ss")
                if n == 4 and k + 1 < len(GROUPS):
                    stage_e(GROUPS[k + 1][0], "ss")
                if n == 6 and g_now is not None:
                    stage_q(g_now)
                mm(bk[0], bk[1], bk[2])
                add_store(bk[0], bk[1], bk[2])
